import numpy as np
import ml_dtypes


def mxq(x, axis, fmt="e4m3"):
    dtype, down = {"e4m3": (ml_dtypes.float8_e4m3fn, 7), "e5m2": (ml_dtypes.float8_e5m2, 14)}[fmt]
    v = np.moveaxis(np.asarray(x, np.float32).astype(ml_dtypes.bfloat16).astype(np.float64), axis, -1)
    blocks = v.reshape(v.shape[:-1] + (-1, 32))
    amax = np.abs(blocks).max(-1, keepdims=True)
    byte = np.maximum(np.where(amax > 0, np.frexp(amax)[1] - 1 + 127, 0) - down, 1)
    scale = np.exp2(byte - 127.0)
    codes = (blocks / scale).astype(np.float32).astype(dtype).astype(np.float64)
    return np.moveaxis((codes * scale).reshape(v.shape), -1, axis)


WIDE = False


def mx_kscale(k):
    if not WIDE:
        return np.ones(k)
    levels = np.array([10, -10, 5, -5, 0])
    a = np.random.permutation(np.resize(levels, k // 512 * 4)).reshape(k // 512, 4)
    idx = np.arange(k)
    return np.exp2(a[idx // 512, idx % 128 // 32])


BF16 = ml_dtypes.bfloat16


def bf(x):
    return np.asarray(x, np.float32).astype(BF16)


def f64(x):
    return np.asarray(x).astype(np.float64)


B, D, MID, NH = 512, 2048, 2048, 4
HALF = D // 2


def setup_inputs():
    s, t = mx_kscale(MID), mx_kscale(MID)
    return {"h": bf(np.maximum(np.random.standard_normal((B, MID)), 0.0) * s),
            "x": bf(np.random.standard_normal((B, D))),
            "w_h": bf(np.random.standard_normal((MID, MID)) * np.sqrt(2.0 / MID) / s[:, None] * t),
            "b_h": bf(np.random.standard_normal(MID) * 0.3 * t),
            "w_out": bf(np.random.standard_normal((MID, HALF)) * np.sqrt(2.0 / MID) / t[:, None]),
            "b_out": bf(np.random.standard_normal(HALF) * 0.3)}


def reference(h, x, w_h, b_h, w_out, b_out):
    xr = f64(x).reshape(B, HALF, 2)
    x1, x2 = xr[:, :, 0], xr[:, :, 1]
    g = np.maximum((mxq(f64(h), 1, "e4m3") @ mxq(f64(w_h), 0, "e4m3")) + f64(b_h), 0.0)
    shift = (mxq(g, 1, "e4m3") @ mxq(f64(w_out), 0, "e4m3")) + f64(b_out)
    return np.stack((x1 + shift, x2), axis=2).reshape(B, D)

@@ -1,0 +1,219 @@
+from contextlib import ExitStack
+
+import concourse.mybir as mybir
+from concourse.masks import make_identity
+
+F32 = mybir.dt.float32
+BF16 = mybir.dt.bfloat16
+U32 = mybir.dt.uint32
+U8 = mybir.dt.uint8
+FP8X4 = mybir.dt.float8_e4m3fn_x4
+ACT = mybir.ActivationFunctionType
+ALU = mybir.AluOpType
+
+P = 128
+B = 512
+MID = 2048
+HALF = 1024
+FLOPS = 2 * B * MID * MID + 2 * B * MID * HALF
+
+WH_V_COLS = 576
+WO_V_PASSES = 1
+RAW_BUFS = 6
+
+
+def regroup(engine_copy, dst, src):
+    engine_copy(
+        out=dst.rearrange("p (c i t) -> p c t i", i=4, t=4),
+        in_=src.rearrange("p t (c i) -> p c t i", i=4),
+    )
+
+
+def tile_additivecoupling_pa_kernel(tc, h, x, w_h, b_h, w_out, b_out, out):
+    nc = tc.nc
+    with ExitStack() as ctx:
+        const = ctx.enter_context(tc.tile_pool(name="const", bufs=1))
+        keep = ctx.enter_context(tc.tile_pool(name="keep", bufs=1))
+        act = ctx.enter_context(tc.tile_pool(name="act", bufs=4))
+        rawp = ctx.enter_context(tc.tile_pool(name="rawp", bufs=RAW_BUFS))
+        stagep = ctx.enter_context(tc.tile_pool(name="stagep", bufs=3))
+        grp = ctx.enter_context(tc.tile_pool(name="grp", bufs=4))
+        gpp = ctx.enter_context(tc.tile_pool(name="gpp", bufs=2))
+        stp = ctx.enter_context(tc.tile_pool(name="stp", bufs=4))
+        outp = ctx.enter_context(tc.tile_pool(name="outp", bufs=6))
+        ps = ctx.enter_context(tc.psum_pool(name="ps", bufs=8))
+
+        h_codes = keep.tile([P, 4, B], U32, name="h_codes", align_bytes=64)
+        h_scales = keep.tile([P, 4, B], U8, name="h_scales", align_bytes=64)
+        wh_codes = keep.tile([P, 4, MID], U32, name="wh_codes", align_bytes=64)
+        wh_scales = keep.tile([P, 4, MID], U8, name="wh_scales", align_bytes=64)
+        g_codes = keep.tile([P, 4, B], U32, name="g_codes", align_bytes=64)
+        g_scales = keep.tile([P, 4, B], U8, name="g_scales", align_bytes=64)
+        wo_codes = keep.tile([P, 4, HALF], U32, name="wo_codes", align_bytes=64)
+        wo_scales = keep.tile([P, 4, HALF], U8, name="wo_scales", align_bytes=64)
+
+        raw = {}
+
+        def load_raw(i):
+            if i >= 12:
+                return
+            t = rawp.tile([P, 4, HALF], BF16, name="raw%d" % i, tag="raw")
+            raw[i] = t
+            if i < 8:
+                hh, c = divmod(i, 4)
+                src = w_h[512 * c : 512 * c + 512, HALF * hh : HALF * hh + HALF]
+                nc.sync.dma_start(out=t[:], in_=src.rearrange("(p j) w -> p j w", j=4))
+            else:
+                g = i - 8
+                src = w_out[512 * g : 512 * g + 512, :]
+                nc.sync.dma_start(out=t[:], in_=src.rearrange("(t p) n -> p t n", p=P))
+
+        load_raw(0)
+        load_raw(1)
+        h_sb = []
+        for bt in range(4):
+            t = act.tile([P, MID], BF16, name="h%d" % bt, tag="act")
+            nc.sync.dma_start(out=t[:], in_=h[P * bt : P * bt + P, :])
+            h_sb.append(t)
+        for i in range(2, RAW_BUFS):
+            load_raw(i)
+
+        ident = const.tile([P, P], F32, name="ident")
+        make_identity(nc, ident[:])
+        spread = const.tile([P, P, 2], F32, name="spread")
+        nc.vector.memset(spread[:], 0.0)
+        nc.vector.tensor_copy(out=spread[:, :, 0], in_=ident[:])
+        bias_rows = const.tile([P, P], BF16, name="bias_rows")
+        nc.vector.memset(bias_rows[:], 0.0)
+        nc.scalar.dma_start(out=bias_rows[0:16, :], in_=b_h.rearrange("(r c) -> r c", c=P))
+        nc.scalar.dma_start(out=bias_rows[16:24, :], in_=b_out.rearrange("(r c) -> r c", c=P))
+        bias_rows32 = const.tile([P, P], F32, name="bias_rows32")
+        nc.vector.tensor_copy(out=bias_rows32[:], in_=bias_rows[:])
+        bias_ps = ps.tile([P, 512], F32, name="bias_ps", tag="bank")
+        nc.tensor.transpose(out=bias_ps[:, 0:P], in_=bias_rows32[:], identity=ident[:])
+        bias = const.tile([P, 24], F32, name="bias")
+        nc.vector.tensor_copy(out=bias[:], in_=bias_ps[:, 0:24])
+
+        gh = []
+        for c in range(4):
+            gh.append(grp.tile([P, 4 * B], BF16, name="gh%d" % c, tag="grp", align_bytes=64))
+        for bh in range(2):
+            for c in range(4):
+                tp = ps.tile([P, 512], F32, name="tp%d_%d" % (bh, c), tag="bank")
+                for u in range(2):
+                    for b2 in range(2):
+                        words = h_sb[2 * bh + b2][:].bitcast(F32).rearrange(
+                            "p (c q u) -> p c u q", c=4, u=2
+                        )
+                        nc.tensor.transpose(
+                            out=tp[:, 256 * u + P * b2 : 256 * u + P * b2 + P],
+                            in_=words[:, c, u, :],
+                            identity=ident[:],
+                        )
+                dst = gh[c][:].bitcast(F32).rearrange("p (b u) -> p b u", u=2)
+                src = tp[:].rearrange("p (u b) -> p b u", u=2)
+                if c % 2 == 0:
+                    nc.scalar.copy(out=dst[:, 256 * bh : 256 * bh + 256, :], in_=src)
+                else:
+                    nc.vector.tensor_copy(out=dst[:, 256 * bh : 256 * bh + 256, :], in_=src)
+        for c in range(4):
+            nc.vector.quantize_mx(
+                out=h_codes[:, c, :].bitcast(FP8X4), scales=h_scales[:, c, :], in_=gh[c][:]
+            )
+
+        x_sb = []
+        for hh in range(2):
+            accs = []
+            for m8 in range(8):
+                accs.append(ps.tile([P, 512], F32, name="acc%d_%d" % (hh, m8), tag="bank"))
+            for c in range(4):
+                i = 4 * hh + c
+                st = stagep.tile([P, 4 * HALF], BF16, name="st%d" % i, tag="stage", align_bytes=64)
+                regroup(nc.vector.tensor_copy, st[:, 0 : 4 * WH_V_COLS], raw[i][:, :, 0:WH_V_COLS])
+                regroup(nc.scalar.copy, st[:, 4 * WH_V_COLS :], raw[i][:, :, WH_V_COLS:])
+                cols = slice(HALF * hh, HALF * hh + HALF)
+                nc.vector.quantize_mx(
+                    out=wh_codes[:, c, cols].bitcast(FP8X4), scales=wh_scales[:, c, cols], in_=st[:]
+                )
+                load_raw(i + RAW_BUFS)
+                for m8 in range(8):
+                    mc = slice(HALF * hh + P * m8, HALF * hh + P * m8 + P)
+                    nc.tensor.matmul_mx(
+                        out=accs[m8][:],
+                        lhsT=wh_codes[:, c, mc].bitcast(FP8X4),
+                        lhsT_scale=wh_scales[:, c, mc],
+                        rhs=h_codes[:, c, :].bitcast(FP8X4),
+                        rhs_scale=h_scales[:, c, :],
+                        start=(c == 0),
+                        stop=(c == 3),
+                    )
+            if hh == 1:
+                for bt in range(4):
+                    t = act.tile([P, MID], BF16, name="x%d" % bt, tag="act")
+                    nc.sync.dma_start(out=t[:], in_=x[P * bt : P * bt + P, :])
+                    x_sb.append(t)
+            for g2 in range(2):
+                g = 2 * hh + g2
+                gp = gpp.tile([P, 4, B], BF16, name="gp%d" % g, tag="gp")
+                for t4 in range(4):
+                    m = 4 * g + t4
+                    nc.scalar.activation(
+                        out=gp[:, t4, :],
+                        in_=accs[4 * g2 + t4][:],
+                        func=ACT.Relu,
+                        bias=bias[:, m : m + 1],
+                        scale=1.0,
+                    )
+                gg = grp.tile([P, 4 * B], BF16, name="gg%d" % g, tag="grp", align_bytes=64)
+                regroup(nc.vector.tensor_copy, gg[:], gp[:])
+                nc.vector.quantize_mx(
+                    out=g_codes[:, g, :].bitcast(FP8X4), scales=g_scales[:, g, :], in_=gg[:]
+                )
+
+        spread2 = spread[:].rearrange("p a e -> p (a e)")
+        for q in range(4):
+            st = stagep.tile([P, 4 * HALF], BF16, name="sq%d" % q, tag="stage", align_bytes=64)
+            for g in range(4):
+                eng = nc.vector.tensor_copy if g < WO_V_PASSES else nc.scalar.copy
+                regroup(eng, st[:, HALF * g : HALF * g + HALF], raw[8 + g][:, :, 256 * q : 256 * q + 256])
+            nc.vector.quantize_mx(
+                out=wo_codes[:, q, :].bitcast(FP8X4), scales=wo_scales[:, q, :], in_=st[:]
+            )
+            sts = []
+            for r in range(2):
+                jt = 2 * q + r
+                acc = ps.tile([P, 512], F32, name="sacc%d" % jt, tag="bank")
+                for g in range(4):
+                    jc = slice(256 * g + P * r, 256 * g + P * r + P)
+                    nc.tensor.matmul_mx(
+                        out=acc[:],
+                        lhsT=wo_codes[:, q, jc].bitcast(FP8X4),
+                        lhsT_scale=wo_scales[:, q, jc],
+                        rhs=g_codes[:, g, :].bitcast(FP8X4),
+                        rhs_scale=g_scales[:, g, :],
+                        start=(g == 0),
+                        stop=(g == 3),
+                    )
+                s_t = stp.tile([P, B], F32, name="sT%d" % jt, tag="sT")
+                nc.scalar.activation(
+                    out=s_t[:],
+                    in_=acc[:],
+                    func=ACT.Identity,
+                    bias=bias[:, 16 + jt : 17 + jt],
+                    scale=1.0,
+                )
+                sts.append(s_t)
+            for bt in range(4):
+                tb = ps.tile([P, 512], F32, name="tb%d_%d" % (q, bt), tag="bank")
+                for r in range(2):
+                    for s in range(2):
+                        nc.tensor.transpose(
+                            out=tb[:, 256 * r + P * s : 256 * r + P * s + P],
+                            in_=sts[r][:, P * bt : P * bt + P],
+                            identity=spread2[:, P * s : P * s + P],
+                        )
+                o = outp.tile([P, 512], F32, name="o%d_%d" % (q, bt), tag="o")
+                nc.vector.tensor_tensor(
+                    out=o[:], in0=tb[:], in1=x_sb[bt][:, 512 * q : 512 * q + 512], op=ALU.add
+                )
+                nc.sync.dma_start(out=out[P * bt : P * bt + P, 512 * q : 512 * q + 512], in_=o[:])

@@ -17,8 +17,10 @@ MID = 2048
 HALF = 1024
 FLOPS = 2 * B * MID * MID + 2 * B * MID * HALF
 
+WH_V_COLS_FIRST = 600
 WH_V_COLS = 576
-WO_V_PASSES = 1
+WH_V_COLS_LATE = 608
+WO_V_PASSES = (2, 2, 2, 1)
 RAW_BUFS = 6
 
 
@@ -39,9 +41,9 @@ def tile_additivecoupling_pa_kernel(tc, h, x, w_h, b_h, w_out, b_out, out):
         stagep = ctx.enter_context(tc.tile_pool(name="stagep", bufs=3))
         grp = ctx.enter_context(tc.tile_pool(name="grp", bufs=4))
         gpp = ctx.enter_context(tc.tile_pool(name="gpp", bufs=2))
-        stp = ctx.enter_context(tc.tile_pool(name="stp", bufs=4))
         outp = ctx.enter_context(tc.tile_pool(name="outp", bufs=6))
         ps = ctx.enter_context(tc.psum_pool(name="ps", bufs=8))
+        ctx.enter_context(tc.manual_schedule())
 
         h_codes = keep.tile([P, 4, B], U32, name="h_codes", align_bytes=64)
         h_scales = keep.tile([P, 4, B], U8, name="h_scales", align_bytes=64)
@@ -53,6 +55,12 @@ def tile_additivecoupling_pa_kernel(tc, h, x, w_h, b_h, w_out, b_out, out):
         wo_scales = keep.tile([P, 4, HALF], U8, name="wo_scales", align_bytes=64)
 
         raw = {}
+        stage = {}
+        accs = {}
+        gp = {}
+        gg = {}
+        x_sb = []
+        h_sb = []
 
         def load_raw(i):
             if i >= 12:
@@ -64,13 +72,143 @@ def tile_additivecoupling_pa_kernel(tc, h, x, w_h, b_h, w_out, b_out, out):
                 src = w_h[512 * c : 512 * c + 512, HALF * hh : HALF * hh + HALF]
                 nc.sync.dma_start(out=t[:], in_=src.rearrange("(p j) w -> p j w", j=4))
             else:
-                g = i - 8
-                src = w_out[512 * g : 512 * g + 512, :]
-                nc.sync.dma_start(out=t[:], in_=src.rearrange("(t p) n -> p t n", p=P))
+                jh, gp2 = divmod(i - 8, 2)
+                src = w_out[1024 * gp2 : 1024 * gp2 + 1024, 512 * jh : 512 * jh + 512]
+                nc.sync.dma_start(
+                    out=t[:].rearrange("p a (b n) -> p (a b) n", b=2),
+                    in_=src.rearrange("(gt p) n -> p gt n", p=P),
+                )
+
+        def regroup_wh(i):
+            vc = WH_V_COLS_FIRST if i < 2 else (WH_V_COLS if i < 5 else WH_V_COLS_LATE)
+            st = stagep.tile([P, 4 * HALF], BF16, name="st%d" % i, tag="stage", align_bytes=64)
+            stage[i] = st
+            regroup(nc.vector.tensor_copy, st[:, 0 : 4 * vc], raw[i][:, :, 0:vc])
+            regroup(nc.scalar.copy, st[:, 4 * vc :], raw[i][:, :, vc:])
+
+        def quantise_wh(i):
+            hh, c = divmod(i, 4)
+            cols = slice(HALF * hh, HALF * hh + HALF)
+            nc.vector.quantize_mx(
+                out=wh_codes[:, c, cols].bitcast(FP8X4), scales=wh_scales[:, c, cols], in_=stage[i][:]
+            )
+            load_raw(i + RAW_BUFS)
+
+        def matmul1(i):
+            hh, c = divmod(i, 4)
+            for m8 in range(8):
+                m = 8 * hh + m8
+                if c == 0:
+                    accs[m] = ps.tile([P, 512], F32, name="acc%d" % m, tag="bank")
+                mc = slice(P * m, P * m + P)
+                nc.tensor.matmul_mx(
+                    out=accs[m][:],
+                    lhsT=wh_codes[:, c, mc].bitcast(FP8X4),
+                    lhsT_scale=wh_scales[:, c, mc],
+                    rhs=h_codes[:, c, :].bitcast(FP8X4),
+                    rhs_scale=h_scales[:, c, :],
+                    start=(c == 0),
+                    stop=(c == 3),
+                )
+
+        def drain_g(m, on_vector):
+            g, t4 = divmod(m, 4)
+            if t4 == 0:
+                gp[g] = gpp.tile([P, 4, B], BF16, name="gp%d" % g, tag="gp")
+            if on_vector:
+                nc.vector.tensor_scalar(
+                    out=gp[g][:, t4, :],
+                    in0=accs[m][:],
+                    scalar1=bias[:, m : m + 1],
+                    scalar2=0.0,
+                    op0=ALU.add,
+                    op1=ALU.max,
+                )
+            else:
+                nc.scalar.activation(
+                    out=gp[g][:, t4, :], in_=accs[m][:], func=ACT.Relu, bias=bias[:, m : m + 1], scale=1.0
+                )
+
+        def regroup_g(g):
+            gg[g] = grp.tile([P, 4 * B], BF16, name="gg%d" % g, tag="grp", align_bytes=64)
+            regroup(nc.vector.tensor_copy, gg[g][:], gp[g][:])
+
+        def quantise_g(g):
+            nc.vector.quantize_mx(
+                out=g_codes[:, g, :].bitcast(FP8X4), scales=g_scales[:, g, :], in_=gg[g][:]
+            )
+
+        def regroup_wo(q):
+            st = stagep.tile([P, 4 * HALF], BF16, name="sq%d" % q, tag="stage", align_bytes=64)
+            stage[8 + q] = st
+            for g in range(4):
+                eng = nc.vector.tensor_copy if g < WO_V_PASSES[q] else nc.scalar.copy
+                piece = raw[8 + 2 * (q // 2) + g // 2][:].rearrange("p a (b n) -> p (a b) n", b=2)
+                rows = slice(4 * (g % 2), 4 * (g % 2) + 4)
+                cols = slice(256 * (q % 2), 256 * (q % 2) + 256)
+                regroup(eng, st[:, HALF * g : HALF * g + HALF], piece[:, rows, cols])
+
+        def quantise_wo(q):
+            nc.vector.quantize_mx(
+                out=wo_codes[:, q, :].bitcast(FP8X4), scales=wo_scales[:, q, :], in_=stage[8 + q][:]
+            )
+
+        banks = {}
+
+        def x_plus_bias(q):
+            for hb in range(2):
+                xb = ps.tile([P, 512], F32, name="xb%d_%d" % (q, hb), tag="bank")
+                for k in range(2):
+                    cols = slice(256 * k, 256 * k + 256)
+                    nc.tensor.matmul(
+                        out=xb[:, cols],
+                        lhsT=ident_bf[:],
+                        rhs=x_sb[2 * hb + k][:].rearrange("p (j e) -> p e j", e=2)[:, 0, 256 * q : 256 * q + 256],
+                        start=True,
+                        stop=False,
+                    )
+                    nc.tensor.matmul(
+                        out=xb[:, cols],
+                        lhsT=ones_bf[:],
+                        rhs=brow[:, 256 * q : 256 * q + 256],
+                        start=False,
+                        stop=True,
+                    )
+                nc.scalar.copy(out=tplane[q % 2][:, 0, 512 * hb : 512 * hb + 512], in_=xb[:])
+
+        def matmul2(q, bt):
+            bank = ps.tile([P, 512], F32, name="sh%d_%d" % (q, bt), tag="bank")
+            banks[bt] = bank
+            nc.tensor.matmul(
+                out=bank[:, 256:512],
+                lhsT=ident_bf[:],
+                rhs=x_sb[bt][:].rearrange("p (j e) -> p e j", e=2)[:, 1, 256 * q : 256 * q + 256],
+                start=True,
+                stop=True,
+            )
+            for g in range(4):
+                nc.tensor.matmul_mx(
+                    out=bank[:, 0:256],
+                    lhsT=g_codes[:, g, P * bt : P * bt + P].bitcast(FP8X4),
+                    lhsT_scale=g_scales[:, g, P * bt : P * bt + P],
+                    rhs=wo_codes[:, q, 256 * g : 256 * g + 256].bitcast(FP8X4),
+                    rhs_scale=wo_scales[:, q, 256 * g : 256 * g + 256],
+                    start=(g == 0),
+                    stop=(g == 3),
+                )
+
+        def add_and_store(q, bt):
+            o = outp.tile([P, 512], F32, name="o%d_%d" % (q, bt), tag="o")
+            nc.vector.tensor_tensor(
+                out=o[:].rearrange("p (j e) -> p j e", e=2),
+                in0=banks[bt][:].rearrange("p (e j) -> p j e", e=2),
+                in1=tplane[q % 2][:, :, 256 * bt : 256 * bt + 256].rearrange("p e j -> p j e"),
+                op=ALU.add,
+            )
+            nc.sync.dma_start(out=out[P * bt : P * bt + P, 512 * q : 512 * q + 512], in_=o[:])
 
         load_raw(0)
         load_raw(1)
-        h_sb = []
         for bt in range(4):
             t = act.tile([P, MID], BF16, name="h%d" % bt, tag="act")
             nc.sync.dma_start(out=t[:], in_=h[P * bt : P * bt + P, :])
@@ -80,19 +218,29 @@ def tile_additivecoupling_pa_kernel(tc, h, x, w_h, b_h, w_out, b_out, out):
 
         ident = const.tile([P, P], F32, name="ident")
         make_identity(nc, ident[:])
-        spread = const.tile([P, P, 2], F32, name="spread")
-        nc.vector.memset(spread[:], 0.0)
-        nc.vector.tensor_copy(out=spread[:, :, 0], in_=ident[:])
+        ident_bf = const.tile([P, P], BF16, name="ident_bf")
+        make_identity(nc, ident_bf[:])
+        ones_bf = const.tile([P, P], BF16, name="ones_bf")
+        nc.vector.memset(ones_bf[:], 1.0)
+        brow = const.tile([P, HALF], BF16, name="brow")
+        nc.vector.memset(brow[:], 0.0)
+        nc.scalar.dma_start(out=brow[0:1, :], in_=b_out.rearrange("(o n) -> o n", o=1))
+        tplane = []
+        for k in range(2):
+            tpl = const.tile([P, 2, HALF], F32, name="tplane%d" % k)
+            nc.vector.memset(tpl[:, 1, :], 0.0)
+            tplane.append(tpl)
         bias_rows = const.tile([P, P], BF16, name="bias_rows")
         nc.vector.memset(bias_rows[:], 0.0)
         nc.scalar.dma_start(out=bias_rows[0:16, :], in_=b_h.rearrange("(r c) -> r c", c=P))
-        nc.scalar.dma_start(out=bias_rows[16:24, :], in_=b_out.rearrange("(r c) -> r c", c=P))
         bias_rows32 = const.tile([P, P], F32, name="bias_rows32")
+        bias = const.tile([P, 16], F32, name="bias")
+
+        regroup_wh(0)
+        quantise_wh(0)
+        regroup_wh(1)
+        quantise_wh(1)
         nc.vector.tensor_copy(out=bias_rows32[:], in_=bias_rows[:])
-        bias_ps = ps.tile([P, 512], F32, name="bias_ps", tag="bank")
-        nc.tensor.transpose(out=bias_ps[:, 0:P], in_=bias_rows32[:], identity=ident[:])
-        bias = const.tile([P, 24], F32, name="bias")
-        nc.vector.tensor_copy(out=bias[:], in_=bias_ps[:, 0:24])
 
         gh = []
         for c in range(4):
@@ -111,109 +259,57 @@ def tile_additivecoupling_pa_kernel(tc, h, x, w_h, b_h, w_out, b_out, out):
                             identity=ident[:],
                         )
                 dst = gh[c][:].bitcast(F32).rearrange("p (b u) -> p b u", u=2)
-                src = tp[:].rearrange("p (u b) -> p b u", u=2)
-                if c % 2 == 0:
-                    nc.scalar.copy(out=dst[:, 256 * bh : 256 * bh + 256, :], in_=src)
-                else:
-                    nc.vector.tensor_copy(out=dst[:, 256 * bh : 256 * bh + 256, :], in_=src)
+                nc.scalar.copy(
+                    out=dst[:, 256 * bh : 256 * bh + 256, :], in_=tp[:].rearrange("p (u b) -> p b u", u=2)
+                )
+        bias_ps = ps.tile([P, 512], F32, name="bias_ps", tag="bank")
+        nc.tensor.transpose(out=bias_ps[:, 0:P], in_=bias_rows32[:], identity=ident[:])
         for c in range(4):
             nc.vector.quantize_mx(
                 out=h_codes[:, c, :].bitcast(FP8X4), scales=h_scales[:, c, :], in_=gh[c][:]
             )
+        nc.vector.tensor_copy(out=bias[:], in_=bias_ps[:, 0:16])
+        matmul1(0)
+        matmul1(1)
 
-        x_sb = []
-        for hh in range(2):
-            accs = []
-            for m8 in range(8):
-                accs.append(ps.tile([P, 512], F32, name="acc%d_%d" % (hh, m8), tag="bank"))
-            for c in range(4):
-                i = 4 * hh + c
-                st = stagep.tile([P, 4 * HALF], BF16, name="st%d" % i, tag="stage", align_bytes=64)
-                regroup(nc.vector.tensor_copy, st[:, 0 : 4 * WH_V_COLS], raw[i][:, :, 0:WH_V_COLS])
-                regroup(nc.scalar.copy, st[:, 4 * WH_V_COLS :], raw[i][:, :, WH_V_COLS:])
-                cols = slice(HALF * hh, HALF * hh + HALF)
-                nc.vector.quantize_mx(
-                    out=wh_codes[:, c, cols].bitcast(FP8X4), scales=wh_scales[:, c, cols], in_=st[:]
-                )
-                load_raw(i + RAW_BUFS)
-                for m8 in range(8):
-                    mc = slice(HALF * hh + P * m8, HALF * hh + P * m8 + P)
-                    nc.tensor.matmul_mx(
-                        out=accs[m8][:],
-                        lhsT=wh_codes[:, c, mc].bitcast(FP8X4),
-                        lhsT_scale=wh_scales[:, c, mc],
-                        rhs=h_codes[:, c, :].bitcast(FP8X4),
-                        rhs_scale=h_scales[:, c, :],
-                        start=(c == 0),
-                        stop=(c == 3),
-                    )
-            if hh == 1:
+        regroup_wh(2)
+        for i in range(2, 8):
+            if i + 1 < 8:
+                regroup_wh(i + 1)
+            quantise_wh(i)
+            if i == 3:
                 for bt in range(4):
                     t = act.tile([P, MID], BF16, name="x%d" % bt, tag="act")
                     nc.sync.dma_start(out=t[:], in_=x[P * bt : P * bt + P, :])
                     x_sb.append(t)
-            for g2 in range(2):
-                g = 2 * hh + g2
-                gp = gpp.tile([P, 4, B], BF16, name="gp%d" % g, tag="gp")
-                for t4 in range(4):
-                    m = 4 * g + t4
-                    nc.scalar.activation(
-                        out=gp[:, t4, :],
-                        in_=accs[4 * g2 + t4][:],
-                        func=ACT.Relu,
-                        bias=bias[:, m : m + 1],
-                        scale=1.0,
-                    )
-                gg = grp.tile([P, 4 * B], BF16, name="gg%d" % g, tag="grp", align_bytes=64)
-                regroup(nc.vector.tensor_copy, gg[:], gp[:])
-                nc.vector.quantize_mx(
-                    out=g_codes[:, g, :].bitcast(FP8X4), scales=g_scales[:, g, :], in_=gg[:]
-                )
+            matmul1(i)
+            if i == 4:
+                for m in range(8):
+                    drain_g(m, False)
+            if i == 5:
+                regroup_g(0)
+                quantise_g(0)
+            if i == 6:
+                regroup_g(1)
+                quantise_g(1)
+        regroup_wo(0)
+        quantise_wo(0)
+        for m in range(8, 16):
+            drain_g(m, m in (9, 11))
+            if m == 11:
+                regroup_g(2)
+        quantise_g(2)
+        regroup_g(3)
+        quantise_g(3)
+        regroup_wo(1)
+        quantise_wo(1)
 
-        spread2 = spread[:].rearrange("p a e -> p (a e)")
         for q in range(4):
-            st = stagep.tile([P, 4 * HALF], BF16, name="sq%d" % q, tag="stage", align_bytes=64)
-            for g in range(4):
-                eng = nc.vector.tensor_copy if g < WO_V_PASSES else nc.scalar.copy
-                regroup(eng, st[:, HALF * g : HALF * g + HALF], raw[8 + g][:, :, 256 * q : 256 * q + 256])
-            nc.vector.quantize_mx(
-                out=wo_codes[:, q, :].bitcast(FP8X4), scales=wo_scales[:, q, :], in_=st[:]
-            )
-            sts = []
-            for r in range(2):
-                jt = 2 * q + r
-                acc = ps.tile([P, 512], F32, name="sacc%d" % jt, tag="bank")
-                for g in range(4):
-                    jc = slice(256 * g + P * r, 256 * g + P * r + P)
-                    nc.tensor.matmul_mx(
-                        out=acc[:],
-                        lhsT=wo_codes[:, q, jc].bitcast(FP8X4),
-                        lhsT_scale=wo_scales[:, q, jc],
-                        rhs=g_codes[:, g, :].bitcast(FP8X4),
-                        rhs_scale=g_scales[:, g, :],
-                        start=(g == 0),
-                        stop=(g == 3),
-                    )
-                s_t = stp.tile([P, B], F32, name="sT%d" % jt, tag="sT")
-                nc.scalar.activation(
-                    out=s_t[:],
-                    in_=acc[:],
-                    func=ACT.Identity,
-                    bias=bias[:, 16 + jt : 17 + jt],
-                    scale=1.0,
-                )
-                sts.append(s_t)
+            x_plus_bias(q)
             for bt in range(4):
-                tb = ps.tile([P, 512], F32, name="tb%d_%d" % (q, bt), tag="bank")
-                for r in range(2):
-                    for s in range(2):
-                        nc.tensor.transpose(
-                            out=tb[:, 256 * r + P * s : 256 * r + P * s + P],
-                            in_=sts[r][:, P * bt : P * bt + P],
-                            identity=spread2[:, P * s : P * s + P],
-                        )
-                o = outp.tile([P, 512], F32, name="o%d_%d" % (q, bt), tag="o")
-                nc.vector.tensor_tensor(
-                    out=o[:], in0=tb[:], in1=x_sb[bt][:, 512 * q : 512 * q + 512], op=ALU.add
-                )
-                nc.sync.dma_start(out=out[P * bt : P * bt + P, 512 * q : 512 * q + 512], in_=o[:])
+                matmul2(q, bt)
+            if q + 2 < 4:
+                regroup_wo(q + 2)
+                quantise_wo(q + 2)
+            for bt in range(4):
+                add_and_store(q, bt)

@@ -43,7 +43,6 @@ def tile_additivecoupling_pa_kernel(tc, h, x, w_h, b_h, w_out, b_out, out):
         gpp = ctx.enter_context(tc.tile_pool(name="gpp", bufs=2))
         outp = ctx.enter_context(tc.tile_pool(name="outp", bufs=6))
         ps = ctx.enter_context(tc.psum_pool(name="ps", bufs=8))
-        ctx.enter_context(tc.manual_schedule())
 
         h_codes = keep.tile([P, 4, B], U32, name="h_codes", align_bytes=64)
         h_scales = keep.tile([P, 4, B], U8, name="h_scales", align_bytes=64)

@@ -17,10 +17,8 @@ MID = 2048
 HALF = 1024
 FLOPS = 2 * B * MID * MID + 2 * B * MID * HALF
 
-WH_V_COLS_FIRST = 600
-WH_V_COLS = 576
-WH_V_COLS_LATE = 608
-WO_V_PASSES = (2, 2, 2, 1)
+WH_V_COLS = 592
+WO_V_PASSES = 2
 RAW_BUFS = 6
 
 
@@ -79,7 +77,7 @@ def tile_additivecoupling_pa_kernel(tc, h, x, w_h, b_h, w_out, b_out, out):
                 )
 
         def regroup_wh(i):
-            vc = WH_V_COLS_FIRST if i < 2 else (WH_V_COLS if i < 5 else WH_V_COLS_LATE)
+            vc = WH_V_COLS
             st = stagep.tile([P, 4 * HALF], BF16, name="st%d" % i, tag="stage", align_bytes=64)
             stage[i] = st
             regroup(nc.vector.tensor_copy, st[:, 0 : 4 * vc], raw[i][:, :, 0:vc])
@@ -141,7 +139,7 @@ def tile_additivecoupling_pa_kernel(tc, h, x, w_h, b_h, w_out, b_out, out):
             st = stagep.tile([P, 4 * HALF], BF16, name="sq%d" % q, tag="stage", align_bytes=64)
             stage[8 + q] = st
             for g in range(4):
-                eng = nc.vector.tensor_copy if g < WO_V_PASSES[q] else nc.scalar.copy
+                eng = nc.vector.tensor_copy if g < WO_V_PASSES else nc.scalar.copy
                 piece = raw[8 + 2 * (q // 2) + g // 2][:].rearrange("p a (b n) -> p (a b) n", b=2)
                 rows = slice(4 * (g % 2), 4 * (g % 2) + 4)
                 cols = slice(256 * (q % 2), 256 * (q % 2) + 256)
@@ -294,7 +292,7 @@ def tile_additivecoupling_pa_kernel(tc, h, x, w_h, b_h, w_out, b_out, out):
         regroup_wo(0)
         quantise_wo(0)
         for m in range(8, 16):
-            drain_g(m, m in (9, 11))
+            drain_g(m, False)
             if m == 11:
                 regroup_g(2)
         quantise_g(2)

@@ -12,20 +12,31 @@ ACT = mybir.ActivationFunctionType
 ALU = mybir.AluOpType
 
 P = 128
+PACK = 4
+K_PASS = P * PACK
 B = 512
 MID = 2048
 HALF = 1024
+PASSES = MID // K_PASS
+B_TILES = B // P
+M_TILES = HALF // P
+N_BANKS = 8
+BANK = 512
+N_QUARTERS = 4
+QUARTER = HALF // N_QUARTERS
 FLOPS = 2 * B * MID * MID + 2 * B * MID * HALF
 
-WH_V_COLS = 592
+WH_V_COLS = 544
 WO_V_PASSES = 2
+N_WH_PIECES = 8
+N_PIECES = 12
 RAW_BUFS = 6
 
 
 def regroup(engine_copy, dst, src):
     engine_copy(
-        out=dst.rearrange("p (c i t) -> p c t i", i=4, t=4),
-        in_=src.rearrange("p t (c i) -> p c t i", i=4),
+        out=dst.rearrange("p (v i t) -> p v t i", i=4, t=PACK),
+        in_=src.rearrange("p t (v i) -> p v t i", i=4),
     )
 
 
@@ -34,184 +45,60 @@ def tile_additivecoupling_pa_kernel(tc, h, x, w_h, b_h, w_out, b_out, out):
     with ExitStack() as ctx:
         const = ctx.enter_context(tc.tile_pool(name="const", bufs=1))
         keep = ctx.enter_context(tc.tile_pool(name="keep", bufs=1))
-        act = ctx.enter_context(tc.tile_pool(name="act", bufs=4))
+        act = ctx.enter_context(tc.tile_pool(name="act", bufs=B_TILES))
         rawp = ctx.enter_context(tc.tile_pool(name="rawp", bufs=RAW_BUFS))
         stagep = ctx.enter_context(tc.tile_pool(name="stagep", bufs=3))
-        grp = ctx.enter_context(tc.tile_pool(name="grp", bufs=4))
+        grp = ctx.enter_context(tc.tile_pool(name="grp", bufs=PASSES))
         gpp = ctx.enter_context(tc.tile_pool(name="gpp", bufs=2))
         outp = ctx.enter_context(tc.tile_pool(name="outp", bufs=6))
-        ps = ctx.enter_context(tc.psum_pool(name="ps", bufs=8))
+        ps = ctx.enter_context(tc.psum_pool(name="ps", bufs=N_BANKS))
 
-        h_codes = keep.tile([P, 4, B], U32, name="h_codes", align_bytes=64)
-        h_scales = keep.tile([P, 4, B], U8, name="h_scales", align_bytes=64)
-        wh_codes = keep.tile([P, 4, MID], U32, name="wh_codes", align_bytes=64)
-        wh_scales = keep.tile([P, 4, MID], U8, name="wh_scales", align_bytes=64)
-        g_codes = keep.tile([P, 4, B], U32, name="g_codes", align_bytes=64)
-        g_scales = keep.tile([P, 4, B], U8, name="g_scales", align_bytes=64)
-        wo_codes = keep.tile([P, 4, HALF], U32, name="wo_codes", align_bytes=64)
-        wo_scales = keep.tile([P, 4, HALF], U8, name="wo_scales", align_bytes=64)
+        h_codes = keep.tile([P, PASSES, B], U32, name="h_codes", align_bytes=64)
+        h_scales = keep.tile([P, PASSES, B], U8, name="h_scales", align_bytes=64)
+        wh_codes = keep.tile([P, PASSES, MID], U32, name="wh_codes", align_bytes=64)
+        wh_scales = keep.tile([P, PASSES, MID], U8, name="wh_scales", align_bytes=64)
+        g_codes = keep.tile([P, PASSES, B], U32, name="g_codes", align_bytes=64)
+        g_scales = keep.tile([P, PASSES, B], U8, name="g_scales", align_bytes=64)
+        wo_codes = keep.tile([P, N_QUARTERS, HALF], U32, name="wo_codes", align_bytes=64)
+        wo_scales = keep.tile([P, N_QUARTERS, HALF], U8, name="wo_scales", align_bytes=64)
 
         raw = {}
-        stage = {}
-        accs = {}
-        gp = {}
-        gg = {}
-        x_sb = []
         h_sb = []
+        x_sb = []
 
-        def load_raw(i):
-            if i >= 12:
+        def load_row_tiles(source, name, tiles):
+            for bt in range(B_TILES):
+                rows = act.tile([P, MID], BF16, name="%s%d" % (name, bt), tag="act")
+                nc.sync.dma_start(out=rows[:], in_=source[P * bt : P * bt + P, :])
+                tiles.append(rows)
+
+        def load_piece(i):
+            if i >= N_PIECES:
                 return
-            t = rawp.tile([P, 4, HALF], BF16, name="raw%d" % i, tag="raw")
-            raw[i] = t
-            if i < 8:
-                hh, c = divmod(i, 4)
-                src = w_h[512 * c : 512 * c + 512, HALF * hh : HALF * hh + HALF]
-                nc.sync.dma_start(out=t[:], in_=src.rearrange("(p j) w -> p j w", j=4))
+            piece = rawp.tile([P, PACK, HALF], BF16, name="raw%d" % i, tag="raw")
+            raw[i] = piece
+            if i < N_WH_PIECES:
+                half, c = divmod(i, PASSES)
+                block = w_h[K_PASS * c : K_PASS * c + K_PASS, HALF * half : HALF * half + HALF]
+                nc.sync.dma_start(out=piece[:], in_=block.rearrange("(p t) w -> p t w", t=PACK))
             else:
-                jh, gp2 = divmod(i - 8, 2)
-                src = w_out[1024 * gp2 : 1024 * gp2 + 1024, 512 * jh : 512 * jh + 512]
+                half, d_pair = divmod(i - N_WH_PIECES, 2)
+                block = w_out[
+                    2 * K_PASS * d_pair : 2 * K_PASS * (d_pair + 1),
+                    2 * QUARTER * half : 2 * QUARTER * (half + 1),
+                ]
                 nc.sync.dma_start(
-                    out=t[:].rearrange("p a (b n) -> p (a b) n", b=2),
-                    in_=src.rearrange("(gt p) n -> p gt n", p=P),
+                    out=piece[:].rearrange("p a (b n) -> p (a b) n", b=2),
+                    in_=block.rearrange("(dt p) n -> p dt n", p=P),
                 )
+            if i == N_WH_PIECES + 1:
+                load_row_tiles(x, "x", x_sb)
 
-        def regroup_wh(i):
-            vc = WH_V_COLS
-            st = stagep.tile([P, 4 * HALF], BF16, name="st%d" % i, tag="stage", align_bytes=64)
-            stage[i] = st
-            regroup(nc.vector.tensor_copy, st[:, 0 : 4 * vc], raw[i][:, :, 0:vc])
-            regroup(nc.scalar.copy, st[:, 4 * vc :], raw[i][:, :, vc:])
-
-        def quantise_wh(i):
-            hh, c = divmod(i, 4)
-            cols = slice(HALF * hh, HALF * hh + HALF)
-            nc.vector.quantize_mx(
-                out=wh_codes[:, c, cols].bitcast(FP8X4), scales=wh_scales[:, c, cols], in_=stage[i][:]
-            )
-            load_raw(i + RAW_BUFS)
-
-        def matmul1(i):
-            hh, c = divmod(i, 4)
-            for m8 in range(8):
-                m = 8 * hh + m8
-                if c == 0:
-                    accs[m] = ps.tile([P, 512], F32, name="acc%d" % m, tag="bank")
-                mc = slice(P * m, P * m + P)
-                nc.tensor.matmul_mx(
-                    out=accs[m][:],
-                    lhsT=wh_codes[:, c, mc].bitcast(FP8X4),
-                    lhsT_scale=wh_scales[:, c, mc],
-                    rhs=h_codes[:, c, :].bitcast(FP8X4),
-                    rhs_scale=h_scales[:, c, :],
-                    start=(c == 0),
-                    stop=(c == 3),
-                )
-
-        def drain_g(m, on_vector):
-            g, t4 = divmod(m, 4)
-            if t4 == 0:
-                gp[g] = gpp.tile([P, 4, B], BF16, name="gp%d" % g, tag="gp")
-            if on_vector:
-                nc.vector.tensor_scalar(
-                    out=gp[g][:, t4, :],
-                    in0=accs[m][:],
-                    scalar1=bias[:, m : m + 1],
-                    scalar2=0.0,
-                    op0=ALU.add,
-                    op1=ALU.max,
-                )
-            else:
-                nc.scalar.activation(
-                    out=gp[g][:, t4, :], in_=accs[m][:], func=ACT.Relu, bias=bias[:, m : m + 1], scale=1.0
-                )
-
-        def regroup_g(g):
-            gg[g] = grp.tile([P, 4 * B], BF16, name="gg%d" % g, tag="grp", align_bytes=64)
-            regroup(nc.vector.tensor_copy, gg[g][:], gp[g][:])
-
-        def quantise_g(g):
-            nc.vector.quantize_mx(
-                out=g_codes[:, g, :].bitcast(FP8X4), scales=g_scales[:, g, :], in_=gg[g][:]
-            )
-
-        def regroup_wo(q):
-            st = stagep.tile([P, 4 * HALF], BF16, name="sq%d" % q, tag="stage", align_bytes=64)
-            stage[8 + q] = st
-            for g in range(4):
-                eng = nc.vector.tensor_copy if g < WO_V_PASSES else nc.scalar.copy
-                piece = raw[8 + 2 * (q // 2) + g // 2][:].rearrange("p a (b n) -> p (a b) n", b=2)
-                rows = slice(4 * (g % 2), 4 * (g % 2) + 4)
-                cols = slice(256 * (q % 2), 256 * (q % 2) + 256)
-                regroup(eng, st[:, HALF * g : HALF * g + HALF], piece[:, rows, cols])
-
-        def quantise_wo(q):
-            nc.vector.quantize_mx(
-                out=wo_codes[:, q, :].bitcast(FP8X4), scales=wo_scales[:, q, :], in_=stage[8 + q][:]
-            )
-
-        banks = {}
-
-        def x_plus_bias(q):
-            for hb in range(2):
-                xb = ps.tile([P, 512], F32, name="xb%d_%d" % (q, hb), tag="bank")
-                for k in range(2):
-                    cols = slice(256 * k, 256 * k + 256)
-                    nc.tensor.matmul(
-                        out=xb[:, cols],
-                        lhsT=ident_bf[:],
-                        rhs=x_sb[2 * hb + k][:].rearrange("p (j e) -> p e j", e=2)[:, 0, 256 * q : 256 * q + 256],
-                        start=True,
-                        stop=False,
-                    )
-                    nc.tensor.matmul(
-                        out=xb[:, cols],
-                        lhsT=ones_bf[:],
-                        rhs=brow[:, 256 * q : 256 * q + 256],
-                        start=False,
-                        stop=True,
-                    )
-                nc.scalar.copy(out=tplane[q % 2][:, 0, 512 * hb : 512 * hb + 512], in_=xb[:])
-
-        def matmul2(q, bt):
-            bank = ps.tile([P, 512], F32, name="sh%d_%d" % (q, bt), tag="bank")
-            banks[bt] = bank
-            nc.tensor.matmul(
-                out=bank[:, 256:512],
-                lhsT=ident_bf[:],
-                rhs=x_sb[bt][:].rearrange("p (j e) -> p e j", e=2)[:, 1, 256 * q : 256 * q + 256],
-                start=True,
-                stop=True,
-            )
-            for g in range(4):
-                nc.tensor.matmul_mx(
-                    out=bank[:, 0:256],
-                    lhsT=g_codes[:, g, P * bt : P * bt + P].bitcast(FP8X4),
-                    lhsT_scale=g_scales[:, g, P * bt : P * bt + P],
-                    rhs=wo_codes[:, q, 256 * g : 256 * g + 256].bitcast(FP8X4),
-                    rhs_scale=wo_scales[:, q, 256 * g : 256 * g + 256],
-                    start=(g == 0),
-                    stop=(g == 3),
-                )
-
-        def add_and_store(q, bt):
-            o = outp.tile([P, 512], F32, name="o%d_%d" % (q, bt), tag="o")
-            nc.vector.tensor_tensor(
-                out=o[:].rearrange("p (j e) -> p j e", e=2),
-                in0=banks[bt][:].rearrange("p (e j) -> p j e", e=2),
-                in1=tplane[q % 2][:, :, 256 * bt : 256 * bt + 256].rearrange("p e j -> p j e"),
-                op=ALU.add,
-            )
-            nc.sync.dma_start(out=out[P * bt : P * bt + P, 512 * q : 512 * q + 512], in_=o[:])
-
-        load_raw(0)
-        load_raw(1)
-        for bt in range(4):
-            t = act.tile([P, MID], BF16, name="h%d" % bt, tag="act")
-            nc.sync.dma_start(out=t[:], in_=h[P * bt : P * bt + P, :])
-            h_sb.append(t)
+        load_piece(0)
+        load_piece(1)
+        load_row_tiles(h, "h", h_sb)
         for i in range(2, RAW_BUFS):
-            load_raw(i)
+            load_piece(i)
 
         ident = const.tile([P, P], F32, name="ident")
         make_identity(nc, ident[:])
@@ -219,94 +106,150 @@ def tile_additivecoupling_pa_kernel(tc, h, x, w_h, b_h, w_out, b_out, out):
         make_identity(nc, ident_bf[:])
         ones_bf = const.tile([P, P], BF16, name="ones_bf")
         nc.vector.memset(ones_bf[:], 1.0)
-        brow = const.tile([P, HALF], BF16, name="brow")
-        nc.vector.memset(brow[:], 0.0)
-        nc.scalar.dma_start(out=brow[0:1, :], in_=b_out.rearrange("(o n) -> o n", o=1))
-        tplane = []
-        for k in range(2):
-            tpl = const.tile([P, 2, HALF], F32, name="tplane%d" % k)
-            nc.vector.memset(tpl[:, 1, :], 0.0)
-            tplane.append(tpl)
-        bias_rows = const.tile([P, P], BF16, name="bias_rows")
-        nc.vector.memset(bias_rows[:], 0.0)
-        nc.scalar.dma_start(out=bias_rows[0:16, :], in_=b_h.rearrange("(r c) -> r c", c=P))
-        bias_rows32 = const.tile([P, P], F32, name="bias_rows32")
-        bias = const.tile([P, 16], F32, name="bias")
+        b_out_row = const.tile([P, HALF], BF16, name="b_out_row")
+        nc.vector.memset(b_out_row[:], 0.0)
+        nc.scalar.dma_start(out=b_out_row[0:1, :], in_=b_out.rearrange("(o n) -> o n", o=1))
+        x_even = []
+        for n in range(2):
+            planes = const.tile([P, 2, HALF], F32, name="x_even%d" % n)
+            nc.vector.memset(planes[:, 1, :], 0.0)
+            x_even.append(planes)
+        b_h_rows = const.tile([P, P], BF16, name="b_h_rows")
+        nc.vector.memset(b_h_rows[:], 0.0)
+        nc.scalar.dma_start(out=b_h_rows[0 : MID // P, :], in_=b_h.rearrange("(r n) -> r n", n=P))
 
-        regroup_wh(0)
-        quantise_wh(0)
-        regroup_wh(1)
-        quantise_wh(1)
-        nc.vector.tensor_copy(out=bias_rows32[:], in_=bias_rows[:])
-
-        gh = []
-        for c in range(4):
-            gh.append(grp.tile([P, 4 * B], BF16, name="gh%d" % c, tag="grp", align_bytes=64))
-        for bh in range(2):
-            for c in range(4):
-                tp = ps.tile([P, 512], F32, name="tp%d_%d" % (bh, c), tag="bank")
+        h_grouped = []
+        for c in range(PASSES):
+            h_grouped.append(grp.tile([P, PACK * B], BF16, name="gh%d" % c, tag="grp", align_bytes=64))
+        for bt_pair in range(B_TILES // 2):
+            for c in range(PASSES):
+                words_t = ps.tile([P, BANK], F32, name="tp%d_%d" % (bt_pair, c), tag="bank")
                 for u in range(2):
                     for b2 in range(2):
-                        words = h_sb[2 * bh + b2][:].bitcast(F32).rearrange(
-                            "p (c q u) -> p c u q", c=4, u=2
+                        words = h_sb[2 * bt_pair + b2][:].bitcast(F32).rearrange(
+                            "p (c q u) -> p c u q", c=PASSES, u=2
                         )
                         nc.tensor.transpose(
-                            out=tp[:, 256 * u + P * b2 : 256 * u + P * b2 + P],
+                            out=words_t[:, 2 * P * u + P * b2 : 2 * P * u + P * b2 + P],
                             in_=words[:, c, u, :],
                             identity=ident[:],
                         )
-                dst = gh[c][:].bitcast(F32).rearrange("p (b u) -> p b u", u=2)
+                grouped_words = h_grouped[c][:].bitcast(F32).rearrange("p (b u) -> p b u", u=2)
                 nc.scalar.copy(
-                    out=dst[:, 256 * bh : 256 * bh + 256, :], in_=tp[:].rearrange("p (u b) -> p b u", u=2)
+                    out=grouped_words[:, 2 * P * bt_pair : 2 * P * (bt_pair + 1), :],
+                    in_=words_t[:].rearrange("p (u b) -> p b u", u=2),
                 )
-        bias_ps = ps.tile([P, 512], F32, name="bias_ps", tag="bank")
-        nc.tensor.transpose(out=bias_ps[:, 0:P], in_=bias_rows32[:], identity=ident[:])
-        for c in range(4):
+        for c in range(PASSES):
             nc.vector.quantize_mx(
-                out=h_codes[:, c, :].bitcast(FP8X4), scales=h_scales[:, c, :], in_=gh[c][:]
+                out=h_codes[:, c, :].bitcast(FP8X4), scales=h_scales[:, c, :], in_=h_grouped[c][:]
             )
-        nc.vector.tensor_copy(out=bias[:], in_=bias_ps[:, 0:16])
-        matmul1(0)
-        matmul1(1)
 
-        regroup_wh(2)
-        for i in range(2, 8):
-            if i + 1 < 8:
-                regroup_wh(i + 1)
-            quantise_wh(i)
-            if i == 3:
-                for bt in range(4):
-                    t = act.tile([P, MID], BF16, name="x%d" % bt, tag="act")
-                    nc.sync.dma_start(out=t[:], in_=x[P * bt : P * bt + P, :])
-                    x_sb.append(t)
-            matmul1(i)
-            if i == 4:
-                for m in range(8):
-                    drain_g(m, False)
-            if i == 5:
-                regroup_g(0)
-                quantise_g(0)
-            if i == 6:
-                regroup_g(1)
-                quantise_g(1)
-        regroup_wo(0)
-        quantise_wo(0)
-        for m in range(8, 16):
-            drain_g(m, False)
-            if m == 11:
-                regroup_g(2)
-        quantise_g(2)
-        regroup_g(3)
-        quantise_g(3)
-        regroup_wo(1)
-        quantise_wo(1)
+        b_h_rows32 = const.tile([P, P], F32, name="b_h_rows32")
+        nc.vector.tensor_copy(out=b_h_rows32[:], in_=b_h_rows[:])
+        b_h_ps = ps.tile([P, BANK], F32, name="b_h_ps", tag="bank")
+        nc.tensor.transpose(out=b_h_ps[:, 0:P], in_=b_h_rows32[:], identity=ident[:])
+        b_h_col = const.tile([P, MID // P], F32, name="b_h_col")
+        nc.vector.tensor_copy(out=b_h_col[:], in_=b_h_ps[:, 0 : MID // P])
 
-        for q in range(4):
-            x_plus_bias(q)
-            for bt in range(4):
-                matmul2(q, bt)
-            if q + 2 < 4:
-                regroup_wo(q + 2)
-                quantise_wo(q + 2)
-            for bt in range(4):
-                add_and_store(q, bt)
+        for half in range(2):
+            g_sums = []
+            for m in range(M_TILES * half, M_TILES * (half + 1)):
+                g_sums.append(ps.tile([P, BANK], F32, name="acc%d" % m, tag="bank"))
+            for c in range(PASSES):
+                i = PASSES * half + c
+                staged = stagep.tile([P, PACK * HALF], BF16, name="st%d" % i, tag="stage", align_bytes=64)
+                regroup(nc.vector.tensor_copy, staged[:, 0 : PACK * WH_V_COLS], raw[i][:, :, 0:WH_V_COLS])
+                regroup(nc.scalar.copy, staged[:, PACK * WH_V_COLS :], raw[i][:, :, WH_V_COLS:])
+                half_cols = slice(HALF * half, HALF * half + HALF)
+                nc.vector.quantize_mx(
+                    out=wh_codes[:, c, half_cols].bitcast(FP8X4),
+                    scales=wh_scales[:, c, half_cols],
+                    in_=staged[:],
+                )
+                load_piece(i + RAW_BUFS)
+                for m in range(M_TILES * half, M_TILES * (half + 1)):
+                    m_cols = slice(P * m, P * m + P)
+                    nc.tensor.matmul_mx(
+                        out=g_sums[m - M_TILES * half][:],
+                        lhsT=wh_codes[:, c, m_cols].bitcast(FP8X4),
+                        lhsT_scale=wh_scales[:, c, m_cols],
+                        rhs=h_codes[:, c, :].bitcast(FP8X4),
+                        rhs_scale=h_scales[:, c, :],
+                        start=(c == 0),
+                        stop=(c == PASSES - 1),
+                    )
+            for d in range(2 * half, 2 * half + 2):
+                g_rows = gpp.tile([P, PACK, B], BF16, name="gp%d" % d, tag="gp")
+                for t in range(PACK):
+                    m = PACK * d + t
+                    nc.scalar.activation(
+                        out=g_rows[:, t, :],
+                        in_=g_sums[m - M_TILES * half][:],
+                        func=ACT.Relu,
+                        bias=b_h_col[:, m : m + 1],
+                        scale=1.0,
+                    )
+                g_grouped = grp.tile([P, PACK * B], BF16, name="gg%d" % d, tag="grp", align_bytes=64)
+                regroup(nc.vector.tensor_copy, g_grouped[:], g_rows[:])
+                nc.vector.quantize_mx(
+                    out=g_codes[:, d, :].bitcast(FP8X4), scales=g_scales[:, d, :], in_=g_grouped[:]
+                )
+
+        def quantise_w_out(q):
+            staged = stagep.tile([P, PACK * HALF], BF16, name="sq%d" % q, tag="stage", align_bytes=64)
+            half, q2 = divmod(q, 2)
+            for d in range(PASSES):
+                d_pair, d2 = divmod(d, 2)
+                piece = raw[N_WH_PIECES + 2 * half + d_pair][:].rearrange("p a (b n) -> p (a b) n", b=2)
+                regroup(
+                    nc.vector.tensor_copy if d < WO_V_PASSES else nc.scalar.copy,
+                    staged[:, HALF * d : HALF * d + HALF],
+                    piece[:, PACK * d2 : PACK * d2 + PACK, QUARTER * q2 : QUARTER * q2 + QUARTER],
+                )
+            nc.vector.quantize_mx(
+                out=wo_codes[:, q, :].bitcast(FP8X4), scales=wo_scales[:, q, :], in_=staged[:]
+            )
+
+        quantise_w_out(0)
+        quantise_w_out(1)
+        for q in range(N_QUARTERS):
+            js = slice(QUARTER * q, QUARTER * q + QUARTER)
+            for bt_pair in range(B_TILES // 2):
+                x_sums = ps.tile([P, BANK], F32, name="xb%d_%d" % (q, bt_pair), tag="bank")
+                for b2 in range(2):
+                    part = slice(QUARTER * b2, QUARTER * b2 + QUARTER)
+                    x_cols = x_sb[2 * bt_pair + b2][:].rearrange("p (j e) -> p e j", e=2)
+                    nc.tensor.matmul(out=x_sums[:, part], lhsT=ident_bf[:], rhs=x_cols[:, 0, js], start=True, stop=False)
+                    nc.tensor.matmul(out=x_sums[:, part], lhsT=ones_bf[:], rhs=b_out_row[:, js], start=False, stop=True)
+                nc.scalar.copy(out=x_even[q % 2][:, 0, BANK * bt_pair : BANK * (bt_pair + 1)], in_=x_sums[:])
+            shifts = []
+            for bt in range(B_TILES):
+                shift = ps.tile([P, BANK], F32, name="sh%d_%d" % (q, bt), tag="bank")
+                shifts.append(shift)
+                x_cols = x_sb[bt][:].rearrange("p (j e) -> p e j", e=2)
+                nc.tensor.matmul(
+                    out=shift[:, QUARTER:BANK], lhsT=ident_bf[:], rhs=x_cols[:, 1, js], start=True, stop=True
+                )
+                bs = slice(P * bt, P * bt + P)
+                for d in range(PASSES):
+                    dj = slice(QUARTER * d, QUARTER * d + QUARTER)
+                    nc.tensor.matmul_mx(
+                        out=shift[:, 0:QUARTER],
+                        lhsT=g_codes[:, d, bs].bitcast(FP8X4),
+                        lhsT_scale=g_scales[:, d, bs],
+                        rhs=wo_codes[:, q, dj].bitcast(FP8X4),
+                        rhs_scale=wo_scales[:, q, dj],
+                        start=(d == 0),
+                        stop=(d == PASSES - 1),
+                    )
+            if q + 2 < N_QUARTERS:
+                quantise_w_out(q + 2)
+            for bt in range(B_TILES):
+                block = outp.tile([P, BANK], F32, name="o%d_%d" % (q, bt), tag="o")
+                nc.vector.tensor_tensor(
+                    out=block[:].rearrange("p (j e) -> p j e", e=2),
+                    in0=shifts[bt][:].rearrange("p (e j) -> p j e", e=2),
+                    in1=x_even[q % 2][:, :, QUARTER * bt : QUARTER * bt + QUARTER].rearrange("p e j -> p j e"),
+                    op=ALU.add,
+                )
+                nc.sync.dma_start(out=out[P * bt : P * bt + P, BANK * q : BANK * q + BANK], in_=block[:])

from contextlib import ExitStack

import concourse.mybir as mybir
from concourse.masks import make_identity

F32 = mybir.dt.float32
BF16 = mybir.dt.bfloat16
U32 = mybir.dt.uint32
U8 = mybir.dt.uint8
FP8X4 = mybir.dt.float8_e4m3fn_x4
ACT = mybir.ActivationFunctionType
ALU = mybir.AluOpType

P = 128
PACK = 4
K_PASS = P * PACK
B = 512
MID = 2048
HALF = 1024
PASSES = MID // K_PASS
B_TILES = B // P
M_TILES = HALF // P
N_BANKS = 8
BANK = 512
N_QUARTERS = 4
QUARTER = HALF // N_QUARTERS
FLOPS = 2 * B * MID * MID + 2 * B * MID * HALF

WH_V_COLS = 544
WO_V_PASSES = 2
N_WH_PIECES = 8
N_PIECES = 12
RAW_BUFS = 6


def regroup(engine_copy, dst, src):
    engine_copy(
        out=dst.rearrange("p (v i t) -> p v t i", i=4, t=PACK),
        in_=src.rearrange("p t (v i) -> p v t i", i=4),
    )


def tile_additivecoupling_pa_kernel(tc, h, x, w_h, b_h, w_out, b_out, out):
    nc = tc.nc
    with ExitStack() as ctx:
        const = ctx.enter_context(tc.tile_pool(name="const", bufs=1))
        keep = ctx.enter_context(tc.tile_pool(name="keep", bufs=1))
        act = ctx.enter_context(tc.tile_pool(name="act", bufs=B_TILES))
        rawp = ctx.enter_context(tc.tile_pool(name="rawp", bufs=RAW_BUFS))
        stagep = ctx.enter_context(tc.tile_pool(name="stagep", bufs=3))
        grp = ctx.enter_context(tc.tile_pool(name="grp", bufs=PASSES))
        gpp = ctx.enter_context(tc.tile_pool(name="gpp", bufs=2))
        outp = ctx.enter_context(tc.tile_pool(name="outp", bufs=6))
        ps = ctx.enter_context(tc.psum_pool(name="ps", bufs=N_BANKS))

        h_codes = keep.tile([P, PASSES, B], U32, name="h_codes", align_bytes=64)
        h_scales = keep.tile([P, PASSES, B], U8, name="h_scales", align_bytes=64)
        wh_codes = keep.tile([P, PASSES, MID], U32, name="wh_codes", align_bytes=64)
        wh_scales = keep.tile([P, PASSES, MID], U8, name="wh_scales", align_bytes=64)
        g_codes = keep.tile([P, PASSES, B], U32, name="g_codes", align_bytes=64)
        g_scales = keep.tile([P, PASSES, B], U8, name="g_scales", align_bytes=64)
        wo_codes = keep.tile([P, N_QUARTERS, HALF], U32, name="wo_codes", align_bytes=64)
        wo_scales = keep.tile([P, N_QUARTERS, HALF], U8, name="wo_scales", align_bytes=64)

        raw = {}
        h_sb = []
        x_sb = []

        def load_row_tiles(source, name, tiles):
            for bt in range(B_TILES):
                rows = act.tile([P, MID], BF16, name="%s%d" % (name, bt), tag="act")
                nc.sync.dma_start(out=rows[:], in_=source[P * bt : P * bt + P, :])
                tiles.append(rows)

        def load_piece(i):
            if i >= N_PIECES:
                return
            piece = rawp.tile([P, PACK, HALF], BF16, name="raw%d" % i, tag="raw")
            raw[i] = piece
            if i < N_WH_PIECES:
                half, c = divmod(i, PASSES)
                block = w_h[K_PASS * c : K_PASS * c + K_PASS, HALF * half : HALF * half + HALF]
                nc.sync.dma_start(out=piece[:], in_=block.rearrange("(p t) w -> p t w", t=PACK))
            else:
                half, d_pair = divmod(i - N_WH_PIECES, 2)
                block = w_out[
                    2 * K_PASS * d_pair : 2 * K_PASS * (d_pair + 1),
                    2 * QUARTER * half : 2 * QUARTER * (half + 1),
                ]
                nc.sync.dma_start(
                    out=piece[:].rearrange("p a (b n) -> p (a b) n", b=2),
                    in_=block.rearrange("(dt p) n -> p dt n", p=P),
                )
            if i == N_WH_PIECES + 1:
                load_row_tiles(x, "x", x_sb)

        load_piece(0)
        load_piece(1)
        load_row_tiles(h, "h", h_sb)
        for i in range(2, RAW_BUFS):
            load_piece(i)

        ident = const.tile([P, P], F32, name="ident")
        make_identity(nc, ident[:])
        ident_bf = const.tile([P, P], BF16, name="ident_bf")
        make_identity(nc, ident_bf[:])
        ones_bf = const.tile([P, P], BF16, name="ones_bf")
        nc.vector.memset(ones_bf[:], 1.0)
        b_out_row = const.tile([P, HALF], BF16, name="b_out_row")
        nc.vector.memset(b_out_row[:], 0.0)
        nc.scalar.dma_start(out=b_out_row[0:1, :], in_=b_out.rearrange("(o n) -> o n", o=1))
        x_even = []
        for n in range(2):
            planes = const.tile([P, 2, HALF], F32, name="x_even%d" % n)
            nc.vector.memset(planes[:, 1, :], 0.0)
            x_even.append(planes)
        b_h_rows = const.tile([P, P], BF16, name="b_h_rows")
        nc.vector.memset(b_h_rows[:], 0.0)
        nc.scalar.dma_start(out=b_h_rows[0 : MID // P, :], in_=b_h.rearrange("(r n) -> r n", n=P))

        h_grouped = []
        for c in range(PASSES):
            h_grouped.append(grp.tile([P, PACK * B], BF16, name="gh%d" % c, tag="grp", align_bytes=64))
        for bt_pair in range(B_TILES // 2):
            for c in range(PASSES):
                words_t = ps.tile([P, BANK], F32, name="tp%d_%d" % (bt_pair, c), tag="bank")
                for u in range(2):
                    for b2 in range(2):
                        words = h_sb[2 * bt_pair + b2][:].bitcast(F32).rearrange(
                            "p (c q u) -> p c u q", c=PASSES, u=2
                        )
                        nc.tensor.transpose(
                            out=words_t[:, 2 * P * u + P * b2 : 2 * P * u + P * b2 + P],
                            in_=words[:, c, u, :],
                            identity=ident[:],
                        )
                grouped_words = h_grouped[c][:].bitcast(F32).rearrange("p (b u) -> p b u", u=2)
                nc.scalar.copy(
                    out=grouped_words[:, 2 * P * bt_pair : 2 * P * (bt_pair + 1), :],
                    in_=words_t[:].rearrange("p (u b) -> p b u", u=2),
                )
        for c in range(PASSES):
            nc.vector.quantize_mx(
                out=h_codes[:, c, :].bitcast(FP8X4), scales=h_scales[:, c, :], in_=h_grouped[c][:]
            )

        b_h_rows32 = const.tile([P, P], F32, name="b_h_rows32")
        nc.vector.tensor_copy(out=b_h_rows32[:], in_=b_h_rows[:])
        b_h_ps = ps.tile([P, BANK], F32, name="b_h_ps", tag="bank")
        nc.tensor.transpose(out=b_h_ps[:, 0:P], in_=b_h_rows32[:], identity=ident[:])
        b_h_col = const.tile([P, MID // P], F32, name="b_h_col")
        nc.vector.tensor_copy(out=b_h_col[:], in_=b_h_ps[:, 0 : MID // P])

        for half in range(2):
            g_sums = []
            for m in range(M_TILES * half, M_TILES * (half + 1)):
                g_sums.append(ps.tile([P, BANK], F32, name="acc%d" % m, tag="bank"))
            for c in range(PASSES):
                i = PASSES * half + c
                staged = stagep.tile([P, PACK * HALF], BF16, name="st%d" % i, tag="stage", align_bytes=64)
                regroup(nc.vector.tensor_copy, staged[:, 0 : PACK * WH_V_COLS], raw[i][:, :, 0:WH_V_COLS])
                regroup(nc.scalar.copy, staged[:, PACK * WH_V_COLS :], raw[i][:, :, WH_V_COLS:])
                half_cols = slice(HALF * half, HALF * half + HALF)
                nc.vector.quantize_mx(
                    out=wh_codes[:, c, half_cols].bitcast(FP8X4),
                    scales=wh_scales[:, c, half_cols],
                    in_=staged[:],
                )
                load_piece(i + RAW_BUFS)
                for m in range(M_TILES * half, M_TILES * (half + 1)):
                    m_cols = slice(P * m, P * m + P)
                    nc.tensor.matmul_mx(
                        out=g_sums[m - M_TILES * half][:],
                        lhsT=wh_codes[:, c, m_cols].bitcast(FP8X4),
                        lhsT_scale=wh_scales[:, c, m_cols],
                        rhs=h_codes[:, c, :].bitcast(FP8X4),
                        rhs_scale=h_scales[:, c, :],
                        start=(c == 0),
                        stop=(c == PASSES - 1),
                    )
            for d in range(2 * half, 2 * half + 2):
                g_rows = gpp.tile([P, PACK, B], BF16, name="gp%d" % d, tag="gp")
                for t in range(PACK):
                    m = PACK * d + t
                    nc.scalar.activation(
                        out=g_rows[:, t, :],
                        in_=g_sums[m - M_TILES * half][:],
                        func=ACT.Relu,
                        bias=b_h_col[:, m : m + 1],
                        scale=1.0,
                    )
                g_grouped = grp.tile([P, PACK * B], BF16, name="gg%d" % d, tag="grp", align_bytes=64)
                regroup(nc.vector.tensor_copy, g_grouped[:], g_rows[:])
                nc.vector.quantize_mx(
                    out=g_codes[:, d, :].bitcast(FP8X4), scales=g_scales[:, d, :], in_=g_grouped[:]
                )

        def quantise_w_out(q):
            staged = stagep.tile([P, PACK * HALF], BF16, name="sq%d" % q, tag="stage", align_bytes=64)
            half, q2 = divmod(q, 2)
            for d in range(PASSES):
                d_pair, d2 = divmod(d, 2)
                piece = raw[N_WH_PIECES + 2 * half + d_pair][:].rearrange("p a (b n) -> p (a b) n", b=2)
                regroup(
                    nc.vector.tensor_copy if d < WO_V_PASSES else nc.scalar.copy,
                    staged[:, HALF * d : HALF * d + HALF],
                    piece[:, PACK * d2 : PACK * d2 + PACK, QUARTER * q2 : QUARTER * q2 + QUARTER],
                )
            nc.vector.quantize_mx(
                out=wo_codes[:, q, :].bitcast(FP8X4), scales=wo_scales[:, q, :], in_=staged[:]
            )

        quantise_w_out(0)
        quantise_w_out(1)
        for q in range(N_QUARTERS):
            js = slice(QUARTER * q, QUARTER * q + QUARTER)
            for bt_pair in range(B_TILES // 2):
                x_sums = ps.tile([P, BANK], F32, name="xb%d_%d" % (q, bt_pair), tag="bank")
                for b2 in range(2):
                    part = slice(QUARTER * b2, QUARTER * b2 + QUARTER)
                    x_cols = x_sb[2 * bt_pair + b2][:].rearrange("p (j e) -> p e j", e=2)
                    nc.tensor.matmul(out=x_sums[:, part], lhsT=ident_bf[:], rhs=x_cols[:, 0, js], start=True, stop=False)
                    nc.tensor.matmul(out=x_sums[:, part], lhsT=ones_bf[:], rhs=b_out_row[:, js], start=False, stop=True)
                nc.scalar.copy(out=x_even[q % 2][:, 0, BANK * bt_pair : BANK * (bt_pair + 1)], in_=x_sums[:])
            shifts = []
            for bt in range(B_TILES):
                shift = ps.tile([P, BANK], F32, name="sh%d_%d" % (q, bt), tag="bank")
                shifts.append(shift)
                x_cols = x_sb[bt][:].rearrange("p (j e) -> p e j", e=2)
                nc.tensor.matmul(
                    out=shift[:, QUARTER:BANK], lhsT=ident_bf[:], rhs=x_cols[:, 1, js], start=True, stop=True
                )
                bs = slice(P * bt, P * bt + P)
                for d in range(PASSES):
                    dj = slice(QUARTER * d, QUARTER * d + QUARTER)
                    nc.tensor.matmul_mx(
                        out=shift[:, 0:QUARTER],
                        lhsT=g_codes[:, d, bs].bitcast(FP8X4),
                        lhsT_scale=g_scales[:, d, bs],
                        rhs=wo_codes[:, q, dj].bitcast(FP8X4),
                        rhs_scale=wo_scales[:, q, dj],
                        start=(d == 0),
                        stop=(d == PASSES - 1),
                    )
            if q + 2 < N_QUARTERS:
                quantise_w_out(q + 2)
            for bt in range(B_TILES):
                block = outp.tile([P, BANK], F32, name="o%d_%d" % (q, bt), tag="o")
                nc.vector.tensor_tensor(
                    out=block[:].rearrange("p (j e) -> p j e", e=2),
                    in0=shifts[bt][:].rearrange("p (e j) -> p j e", e=2),
                    in1=x_even[q % 2][:, :, QUARTER * bt : QUARTER * bt + QUARTER].rearrange("p e j -> p j e"),
                    op=ALU.add,
                )
                nc.sync.dma_start(out=out[P * bt : P * bt + P, BANK * q : BANK * q + BANK], in_=block[:])
